import numpy as np
import ml_dtypes


def mxq(x, axis, fmt="e4m3"):
    dtype, down = {"e4m3": (ml_dtypes.float8_e4m3fn, 7), "e5m2": (ml_dtypes.float8_e5m2, 14)}[fmt]
    v = np.moveaxis(np.asarray(x, np.float32).astype(ml_dtypes.bfloat16).astype(np.float64), axis, -1)
    blocks = v.reshape(v.shape[:-1] + (-1, 32))
    amax = np.abs(blocks).max(-1, keepdims=True)
    byte = np.maximum(np.where(amax > 0, np.frexp(amax)[1] - 1 + 127, 0) - down, 1)
    scale = np.exp2(byte - 127.0)
    codes = (blocks / scale).astype(np.float32).astype(dtype).astype(np.float64)
    return np.moveaxis((codes * scale).reshape(v.shape), -1, axis)


WIDE = False


def mx_kscale(k):
    if not WIDE:
        return np.ones(k)
    levels = np.array([20, -20, 10, -10, 0])
    a = np.random.permutation(np.resize(levels, k // 512 * 4)).reshape(k // 512, 4)
    idx = np.arange(k)
    return np.exp2(a[idx // 512, idx % 128 // 32])


BF16 = ml_dtypes.bfloat16


def bf(x):
    return np.asarray(x, np.float32).astype(BF16)


def f64(x):
    return np.asarray(x).astype(np.float64)


B, D, I, O = 1024, 4, 512, 512


def setup_inputs():
    s = mx_kscale(B)[:, None]
    x = np.random.standard_normal((B, D * I)) * s
    W = np.random.standard_normal((D * O, D * I)) / np.sqrt(I)
    g = np.random.standard_normal((B, D * O)) * np.exp2(np.random.randint(-12, 1, (B, 1))) / s
    return {"x": bf(x), "W": bf(W), "grad_out": bf(g)}


def reference(x, W, grad_out):
    xb = f64(x).reshape(B, D, I)
    gb = f64(grad_out).reshape(B, D, O)
    xq = mxq(xb, 0, "e4m3")
    gq = mxq(gb, 0, "e5m2")
    gWb = gq.transpose(1, 2, 0) @ xq.transpose(1, 0, 2)
    out = np.zeros((D, O, D, I))
    for d in range(D):
        out[d, :, d, :] = gWb[d]
    return out.reshape(D * O, D * I)

@@ -1,0 +1,111 @@
+from contextlib import ExitStack
+
+import concourse.mybir as mybir
+
+BF16 = mybir.dt.bfloat16
+F32 = mybir.dt.float32
+U32 = mybir.dt.uint32
+U8 = mybir.dt.uint8
+E4M3X4 = mybir.dt.float8_e4m3fn_x4
+E5M2X4 = mybir.dt.float8_e5m2_x4
+
+P = 128
+PACK = 4
+K_PASS = P * PACK
+TOKENS = 1024
+PASSES = TOKENS // K_PASS
+DETS = 4
+BLK = 512
+WIDTH = DETS * BLK
+M_TILES = BLK // P
+
+FLOPS = 2 * DETS * BLK * BLK * TOKENS
+BYTES = 2 * TOKENS * WIDTH * 2 + WIDTH * WIDTH * 4
+
+
+def tile_ensemblelinear_kernel(tc, x, W, grad_out, out):
+    nc = tc.nc
+    with ExitStack() as ctx:
+        keep = ctx.enter_context(tc.tile_pool(name="keep", bufs=1))
+        stage = ctx.enter_context(tc.tile_pool(name="stage", bufs=4))
+        psum = ctx.enter_context(tc.psum_pool(name="psum", bufs=8))
+        ctx.enter_context(tc.manual_schedule())
+
+        src = {"x": x, "g": grad_out}
+        fmt = {"x": E4M3X4, "g": E5M2X4}
+        raw = {}
+        codes = {}
+        scales = {}
+        for who in ("x", "g"):
+            codes[who] = keep.tile([P, PASSES, WIDTH], U32, name="codes_" + who, align_bytes=64)
+            scales[who] = keep.tile([P, PASSES, WIDTH], U8, name="scales_" + who, align_bytes=64)
+        for c in range(PASSES):
+            for who in ("x", "g"):
+                t = keep.tile([P, PACK, WIDTH], BF16, name="raw_%s%d" % (who, c), align_bytes=64)
+                raw[(who, c)] = t
+                nc.sync.dma_start(
+                    out=t[:],
+                    in_=src[who][c * K_PASS : (c + 1) * K_PASS, :].rearrange("(p j) w -> p j w", j=PACK),
+                )
+
+        zero = keep.tile([P, PACK, WIDTH - BLK], F32, name="zero")
+        nc.vector.memset(zero[:], 0.0)
+        for d in range(DETS):
+            rows = out[d * BLK : (d + 1) * BLK, :].rearrange("(p r) c -> p r c", r=PACK)
+            left = d * BLK
+            right = WIDTH - (d + 1) * BLK
+            if left > 0:
+                nc.sync.dma_start(out=rows[:, :, 0:left], in_=zero[:, :, 0:left])
+            if right > 0:
+                nc.sync.dma_start(out=rows[:, :, WIDTH - right : WIDTH], in_=zero[:, :, 0:right])
+
+        def regroup(who, c, d):
+            grouped = stage.tile([P, BLK, PACK], BF16, name="grouped", align_bytes=64)
+            nc.vector.tensor_copy(
+                out=grouped[:].rearrange("p (n i) t -> p n t i", i=4),
+                in_=raw[(who, c)][:, :, d * BLK : (d + 1) * BLK].rearrange("p t (n i) -> p n t i", i=4),
+            )
+            return grouped
+
+        def quantise(who, c, d, grouped):
+            cols = slice(d * BLK, (d + 1) * BLK)
+            nc.vector.quantize_mx(
+                out=codes[who][:, c, cols].bitcast(fmt[who]),
+                scales=scales[who][:, c, cols],
+                in_=grouped[:].rearrange("p w j -> p (w j)"),
+            )
+
+        def block(d):
+            res = stage.tile([P, M_TILES, BLK], F32, name="res")
+            n_cols = slice(d * BLK, (d + 1) * BLK)
+            for t in range(M_TILES):
+                m_cols = slice(d * BLK + t * P, d * BLK + (t + 1) * P)
+                acc = psum.tile([P, BLK], F32, name="acc")
+                for c in range(PASSES):
+                    nc.tensor.matmul_mx(
+                        out=acc[:],
+                        lhsT=codes["g"][:, c, m_cols].bitcast(E5M2X4),
+                        lhsT_scale=scales["g"][:, c, m_cols],
+                        rhs=codes["x"][:, c, n_cols].bitcast(E4M3X4),
+                        rhs_scale=scales["x"][:, c, n_cols],
+                        start=(c == 0),
+                        stop=(c == PASSES - 1),
+                    )
+                nc.scalar.copy(out=res[:, t, :], in_=acc[:])
+            nc.sync.dma_start(
+                out=out[d * BLK : (d + 1) * BLK, n_cols].rearrange("(t m) c -> m t c", t=M_TILES),
+                in_=res[:],
+            )
+
+        chunks = [(who, 0, d) for who in ("x", "g") for d in range(DETS)]
+        chunks += [(who, 1, d) for d in range(DETS) for who in ("x", "g")]
+        waiting = None
+        for chunk in chunks:
+            grouped = regroup(*chunk)
+            if waiting is not None:
+                quantise(*waiting)
+                if waiting[0] == "g" and waiting[1] == PASSES - 1:
+                    block(waiting[2])
+            waiting = chunk + (grouped,)
+        quantise(*waiting)
+        block(waiting[2])

@@ -17,10 +17,14 @@ PASSES = TOKENS // K_PASS
 DETS = 4
 BLK = 512
 WIDTH = DETS * BLK
-M_TILES = BLK // P
+ROWS = BLK // P
 
 FLOPS = 2 * DETS * BLK * BLK * TOKENS
 BYTES = 2 * TOKENS * WIDTH * 2 + WIDTH * WIDTH * 4
+
+ORDER = (1, 2, 3, 0)
+WHOLE = {0: 0, 1: 4, 2: 4, 3: 2}
+STORES = {1: ((0, 1), (1, 2), (2, 4)), 2: ((0, 2), (2, 4)), 3: ((0, 2), (2, 4)), 0: ((0, 4),)}
 
 
 def tile_ensemblelinear_kernel(tc, x, W, grad_out, out):
@@ -48,23 +52,44 @@ def tile_ensemblelinear_kernel(tc, x, W, grad_out, out):
                     in_=src[who][c * K_PASS : (c + 1) * K_PASS, :].rearrange("(p j) w -> p j w", j=PACK),
                 )
 
-        zero = keep.tile([P, PACK, WIDTH - BLK], F32, name="zero")
-        nc.vector.memset(zero[:], 0.0)
+        def out_rows(d):
+            return out[d * BLK : (d + 1) * BLK, :].rearrange("(m r) c -> m r c", r=ROWS)
+
+        whole = {}
+        part = {}
         for d in range(DETS):
-            rows = out[d * BLK : (d + 1) * BLK, :].rearrange("(p r) c -> p r c", r=PACK)
-            left = d * BLK
-            right = WIDTH - (d + 1) * BLK
-            if left > 0:
-                nc.sync.dma_start(out=rows[:, :, 0:left], in_=zero[:, :, 0:left])
-            if right > 0:
-                nc.sync.dma_start(out=rows[:, :, WIDTH - right : WIDTH], in_=zero[:, :, 0:right])
+            if WHOLE[d] > 0:
+                whole[d] = keep.tile([P, WHOLE[d], WIDTH], F32, name="whole_%d" % d)
+            if WHOLE[d] < ROWS:
+                part[d] = keep.tile([P, ROWS - WHOLE[d], BLK], F32, name="part_%d" % d)
+
+        zeros = whole[3][:, 0:2, 0 : 3 * BLK]
+        nc.vector.memset(zeros, 0.0)
+        for d in ORDER:
+            for lo in range(0, WHOLE[d], 2):
+                if d == 3 and lo == 0:
+                    continue
+                for first, width in ((0, d * BLK), ((d + 1) * BLK, WIDTH - (d + 1) * BLK)):
+                    if width > 0:
+                        nc.scalar.copy(out=whole[d][:, lo : lo + 2, first : first + width], in_=zeros[:, :, 0:width])
+        for d in reversed(ORDER):
+            first = BLK if d == 0 else 0
+            for lo in range(WHOLE[d], ROWS, 2):
+                nc.sync.dma_start(out=out_rows(d)[:, lo : lo + 2, first : first + 3 * BLK], in_=zeros)
 
         def regroup(who, c, d):
             grouped = stage.tile([P, BLK, PACK], BF16, name="grouped", align_bytes=64)
-            nc.vector.tensor_copy(
-                out=grouped[:].rearrange("p (n i) t -> p n t i", i=4),
-                in_=raw[(who, c)][:, :, d * BLK : (d + 1) * BLK].rearrange("p t (n i) -> p n t i", i=4),
-            )
+            cols = raw[(who, c)][:, :, d * BLK : (d + 1) * BLK]
+            if who == "x":
+                nc.vector.tensor_copy(
+                    out=grouped[:].rearrange("p (n i) t -> p n t i", i=4),
+                    in_=cols.rearrange("p t (n i) -> p n t i", i=4),
+                )
+            else:
+                nc.vector.tensor_copy(
+                    out=grouped[:].rearrange("p (r m) t -> p m t r", r=ROWS),
+                    in_=cols.rearrange("p t (m r) -> p m t r", r=ROWS),
+                )
             return grouped
 
         def quantise(who, c, d, grouped):
@@ -75,37 +100,61 @@ def tile_ensemblelinear_kernel(tc, x, W, grad_out, out):
                 in_=grouped[:].rearrange("p w j -> p (w j)"),
             )
 
-        def block(d):
-            res = stage.tile([P, M_TILES, BLK], F32, name="res")
+        accs = {}
+
+        def mx_pass(d, c, r):
+            m_cols = slice(d * BLK + r * P, d * BLK + (r + 1) * P)
             n_cols = slice(d * BLK, (d + 1) * BLK)
-            for t in range(M_TILES):
-                m_cols = slice(d * BLK + t * P, d * BLK + (t + 1) * P)
-                acc = psum.tile([P, BLK], F32, name="acc")
-                for c in range(PASSES):
-                    nc.tensor.matmul_mx(
-                        out=acc[:],
-                        lhsT=codes["g"][:, c, m_cols].bitcast(E5M2X4),
-                        lhsT_scale=scales["g"][:, c, m_cols],
-                        rhs=codes["x"][:, c, n_cols].bitcast(E4M3X4),
-                        rhs_scale=scales["x"][:, c, n_cols],
-                        start=(c == 0),
-                        stop=(c == PASSES - 1),
-                    )
-                nc.scalar.copy(out=res[:, t, :], in_=acc[:])
-            nc.sync.dma_start(
-                out=out[d * BLK : (d + 1) * BLK, n_cols].rearrange("(t m) c -> m t c", t=M_TILES),
-                in_=res[:],
+            nc.tensor.matmul_mx(
+                out=accs[(d, r)][:],
+                lhsT=codes["g"][:, c, m_cols].bitcast(E5M2X4),
+                lhsT_scale=scales["g"][:, c, m_cols],
+                rhs=codes["x"][:, c, n_cols].bitcast(E4M3X4),
+                rhs_scale=scales["x"][:, c, n_cols],
+                start=(c == 0),
+                stop=(c == PASSES - 1),
             )
 
-        chunks = [(who, 0, d) for who in ("x", "g") for d in range(DETS)]
-        chunks += [(who, 1, d) for d in range(DETS) for who in ("x", "g")]
-        waiting = None
+        def open_block(d):
+            for r in range(ROWS):
+                accs[(d, r)] = psum.tile([P, BLK], F32, name="acc")
+                mx_pass(d, 0, r)
+
+        def close_block(d):
+            n_cols = slice(d * BLK, (d + 1) * BLK)
+            for r in range(ROWS):
+                mx_pass(d, 1, r)
+                if r < WHOLE[d]:
+                    nc.scalar.copy(out=whole[d][:, r, n_cols], in_=accs[(d, r)][:])
+                else:
+                    nc.scalar.copy(out=part[d][:, r - WHOLE[d], :], in_=accs[(d, r)][:])
+                for lo, hi in STORES[d]:
+                    if hi == r + 1 and hi <= WHOLE[d]:
+                        nc.sync.dma_start(out=out_rows(d)[:, lo:hi, :], in_=whole[d][:, lo:hi, :])
+                    if hi == r + 1 and hi > WHOLE[d]:
+                        nc.sync.dma_start(
+                            out=out_rows(d)[:, lo:hi, n_cols], in_=part[d][:, lo - WHOLE[d] : hi - WHOLE[d], :]
+                        )
+
+        first, second, third, last = ORDER
+        chunks = [("x", 0, first), ("x", 0, second), ("g", 0, first), ("g", 0, second)]
+        chunks += [("x", 1, first), ("x", 1, second), ("x", 0, third), ("g", 1, first), ("g", 1, second)]
+        chunks += [("g", 0, third), ("x", 1, third), ("g", 1, third)]
+        chunks += [("x", 0, last), ("g", 0, last), ("x", 1, last), ("g", 1, last)]
+        urgent = ("g", 1, first)
+
+        def after(who, c, d):
+            if who == "g" and c == 0 and d in (first, second):
+                open_block(d)
+            if who == "g" and c == 1:
+                if d in (third, last):
+                    open_block(d)
+                close_block(d)
+
+        copied = []
         for chunk in chunks:
-            grouped = regroup(*chunk)
-            if waiting is not None:
-                quantise(*waiting)
-                if waiting[0] == "g" and waiting[1] == PASSES - 1:
-                    block(waiting[2])
-            waiting = chunk + (grouped,)
-        quantise(*waiting)
-        block(waiting[2])
+            copied.append(chunk + (regroup(*chunk),))
+            while len(copied) > (0 if chunk in (urgent, chunks[-1]) else 1):
+                oldest = copied.pop(0)
+                quantise(*oldest)
+                after(*oldest[0:3])

@@ -23,8 +23,9 @@ FLOPS = 2 * DETS * BLK * BLK * TOKENS
 BYTES = 2 * TOKENS * WIDTH * 2 + WIDTH * WIDTH * 4
 
 ORDER = (1, 2, 3, 0)
-WHOLE = {0: 0, 1: 4, 2: 4, 3: 2}
-STORES = {1: ((0, 1), (1, 2), (2, 4)), 2: ((0, 2), (2, 4)), 3: ((0, 2), (2, 4)), 0: ((0, 4),)}
+WHOLE = {0: 0, 1: 4, 2: 4, 3: 4}
+STORES = {1: ((0, 1), (1, 2), (2, 4)), 2: ((0, 4),), 3: ((0, 4),), 0: ((0, 4),)}
+URGENT_CUTS = ((0, 1), (1, 2), (2, 4))
 
 
 def tile_ensemblelinear_kernel(tc, x, W, grad_out, out):
@@ -77,27 +78,27 @@ def tile_ensemblelinear_kernel(tc, x, W, grad_out, out):
             for lo in range(WHOLE[d], ROWS, 2):
                 nc.sync.dma_start(out=out_rows(d)[:, lo : lo + 2, first : first + 3 * BLK], in_=zeros)
 
-        def regroup(who, c, d):
+        def regroup(who, c, d, lo, hi):
             grouped = stage.tile([P, BLK, PACK], BF16, name="grouped", align_bytes=64)
-            cols = raw[(who, c)][:, :, d * BLK : (d + 1) * BLK]
+            block = raw[(who, c)][:, :, d * BLK : (d + 1) * BLK]
             if who == "x":
                 nc.vector.tensor_copy(
-                    out=grouped[:].rearrange("p (n i) t -> p n t i", i=4),
-                    in_=cols.rearrange("p t (n i) -> p n t i", i=4),
+                    out=grouped[:, 0 : (hi - lo) * P, :].rearrange("p (n i) t -> p n t i", i=4),
+                    in_=block[:, :, lo * P : hi * P].rearrange("p t (n i) -> p n t i", i=4),
                 )
             else:
                 nc.vector.tensor_copy(
-                    out=grouped[:].rearrange("p (r m) t -> p m t r", r=ROWS),
-                    in_=cols.rearrange("p t (m r) -> p m t r", r=ROWS),
+                    out=grouped[:, 0 : (hi - lo) * P, :].rearrange("p (r m) t -> p m t r", r=hi - lo),
+                    in_=block.rearrange("p t (m r) -> p m t r", r=ROWS)[:, :, :, lo:hi],
                 )
             return grouped
 
-        def quantise(who, c, d, grouped):
-            cols = slice(d * BLK, (d + 1) * BLK)
+        def quantise(who, c, d, lo, hi, grouped):
+            cols = slice(d * BLK + lo * P, d * BLK + hi * P)
             nc.vector.quantize_mx(
                 out=codes[who][:, c, cols].bitcast(fmt[who]),
                 scales=scales[who][:, c, cols],
-                in_=grouped[:].rearrange("p w j -> p (w j)"),
+                in_=grouped[:, 0 : (hi - lo) * P, :].rearrange("p w j -> p (w j)"),
             )
 
         accs = {}
@@ -120,41 +121,47 @@ def tile_ensemblelinear_kernel(tc, x, W, grad_out, out):
                 accs[(d, r)] = psum.tile([P, BLK], F32, name="acc")
                 mx_pass(d, 0, r)
 
-        def close_block(d):
+        def close_rows(d, lo, hi):
             n_cols = slice(d * BLK, (d + 1) * BLK)
-            for r in range(ROWS):
+            for r in range(lo, hi):
                 mx_pass(d, 1, r)
                 if r < WHOLE[d]:
                     nc.scalar.copy(out=whole[d][:, r, n_cols], in_=accs[(d, r)][:])
                 else:
                     nc.scalar.copy(out=part[d][:, r - WHOLE[d], :], in_=accs[(d, r)][:])
-                for lo, hi in STORES[d]:
-                    if hi == r + 1 and hi <= WHOLE[d]:
-                        nc.sync.dma_start(out=out_rows(d)[:, lo:hi, :], in_=whole[d][:, lo:hi, :])
-                    if hi == r + 1 and hi > WHOLE[d]:
-                        nc.sync.dma_start(
-                            out=out_rows(d)[:, lo:hi, n_cols], in_=part[d][:, lo - WHOLE[d] : hi - WHOLE[d], :]
-                        )
+                for a, b in STORES[d]:
+                    if b == r + 1 and b <= WHOLE[d]:
+                        nc.sync.dma_start(out=out_rows(d)[:, a:b, :], in_=whole[d][:, a:b, :])
+                    if b == r + 1 and b > WHOLE[d]:
+                        nc.sync.dma_start(out=out_rows(d)[:, a:b, n_cols], in_=part[d][:, a - WHOLE[d] : b - WHOLE[d], :])
 
         first, second, third, last = ORDER
-        chunks = [("x", 0, first), ("x", 0, second), ("g", 0, first), ("g", 0, second)]
-        chunks += [("x", 1, first), ("x", 1, second), ("x", 0, third), ("g", 1, first), ("g", 1, second)]
-        chunks += [("g", 0, third), ("x", 1, third), ("g", 1, third)]
-        chunks += [("x", 0, last), ("g", 0, last), ("x", 1, last), ("g", 1, last)]
-        urgent = ("g", 1, first)
+        urgent = [("g", 1, first, lo, hi) for lo, hi in URGENT_CUTS]
+        early = [("x", 0, first), ("x", 0, second), ("g", 0, first), ("g", 0, second)]
+        early += [("x", 1, first), ("x", 1, second), ("x", 0, third)]
+        late = [("g", 1, second), ("g", 0, third), ("x", 1, third), ("g", 1, third)]
+        late += [("x", 0, last), ("g", 0, last), ("x", 1, last), ("g", 1, last)]
+        chunks = [chunk + (0, ROWS) for chunk in early] + urgent + [chunk + (0, ROWS) for chunk in late]
 
-        def after(who, c, d):
+        def after(who, c, d, lo, hi):
             if who == "g" and c == 0 and d in (first, second):
                 open_block(d)
             if who == "g" and c == 1:
                 if d in (third, last):
                     open_block(d)
-                close_block(d)
+                close_rows(d, lo, hi)
 
         copied = []
-        for chunk in chunks:
-            copied.append(chunk + (regroup(*chunk),))
-            while len(copied) > (0 if chunk in (urgent, chunks[-1]) else 1):
+
+        def quantise_all_but(n):
+            while len(copied) > n:
                 oldest = copied.pop(0)
                 quantise(*oldest)
-                after(*oldest[0:3])
+                after(*oldest[0:5])
+
+        for chunk in chunks:
+            if chunk in urgent:
+                quantise_all_but(0)
+            copied.append(chunk + (regroup(*chunk),))
+            quantise_all_but(0 if chunk in urgent else 1)
+        quantise_all_but(0)

@@ -137,8 +137,8 @@ def tile_ensemblelinear_kernel(tc, x, W, grad_out, out):
 
         first, second, third, last = ORDER
         urgent = [("g", 1, first, lo, hi) for lo, hi in URGENT_CUTS]
-        early = [("x", 0, first), ("x", 0, second), ("g", 0, first), ("g", 0, second)]
-        early += [("x", 1, first), ("x", 1, second), ("x", 0, third)]
+        early = [("x", 0, first), ("x", 0, second), ("x", 0, third), ("g", 0, first), ("g", 0, second)]
+        early += [("x", 1, first), ("x", 1, second)]
         late = [("g", 1, second), ("g", 0, third), ("x", 1, third), ("g", 1, third)]
         late += [("x", 0, last), ("g", 0, last), ("x", 1, last), ("g", 1, last)]
         chunks = [chunk + (0, ROWS) for chunk in early] + urgent + [chunk + (0, ROWS) for chunk in late]

@@ -23,8 +23,14 @@ FLOPS = 2 * DETS * BLK * BLK * TOKENS
 BYTES = 2 * TOKENS * WIDTH * 2 + WIDTH * WIDTH * 4
 
 ORDER = (1, 2, 3, 0)
-WHOLE = {0: 0, 1: 4, 2: 4, 3: 4}
-STORES = {1: ((0, 1), (1, 2), (2, 4)), 2: ((0, 4),), 3: ((0, 4),), 0: ((0, 4),)}
+CHUNK = ROWS * WIDTH
+AHEAD = {0: (3 * WIDTH + BLK, CHUNK), 1: (3 * WIDTH + 2 * BLK, CHUNK), 2: (0, 2 * BLK), 3: (0, 3 * BLK)}
+STORES = {
+    1: {0: (0, WIDTH), 1: (WIDTH, 2 * WIDTH), 3: (2 * WIDTH, 3 * WIDTH + 2 * BLK)},
+    2: {3: (2 * BLK, CHUNK)},
+    3: {3: (3 * BLK, CHUNK)},
+    0: {3: (0, 3 * WIDTH + BLK)},
+}
 URGENT_CUTS = ((0, 1), (1, 2), (2, 4))
 
 
@@ -53,30 +59,26 @@ def tile_ensemblelinear_kernel(tc, x, W, grad_out, out):
                     in_=src[who][c * K_PASS : (c + 1) * K_PASS, :].rearrange("(p j) w -> p j w", j=PACK),
                 )
 
-        def out_rows(d):
-            return out[d * BLK : (d + 1) * BLK, :].rearrange("(m r) c -> m r c", r=ROWS)
+        def out_chunk(d):
+            return out[d * BLK : (d + 1) * BLK, :].rearrange("(m r) c -> m (r c)", r=ROWS)
 
         whole = {}
-        part = {}
-        for d in range(DETS):
-            if WHOLE[d] > 0:
-                whole[d] = keep.tile([P, WHOLE[d], WIDTH], F32, name="whole_%d" % d)
-            if WHOLE[d] < ROWS:
-                part[d] = keep.tile([P, ROWS - WHOLE[d], BLK], F32, name="part_%d" % d)
+        for d in ORDER[0:3]:
+            whole[d] = keep.tile([P, ROWS, WIDTH], F32, name="whole_%d" % d)
+        whole[ORDER[3]] = whole[ORDER[0]]
 
         zeros = whole[3][:, 0:2, 0 : 3 * BLK]
         nc.vector.memset(zeros, 0.0)
-        for d in ORDER:
-            for lo in range(0, WHOLE[d], 2):
+        for d in ORDER[0:3]:
+            for lo in range(0, ROWS, 2):
                 if d == 3 and lo == 0:
                     continue
                 for first, width in ((0, d * BLK), ((d + 1) * BLK, WIDTH - (d + 1) * BLK)):
                     if width > 0:
                         nc.scalar.copy(out=whole[d][:, lo : lo + 2, first : first + width], in_=zeros[:, :, 0:width])
         for d in reversed(ORDER):
-            first = BLK if d == 0 else 0
-            for lo in range(WHOLE[d], ROWS, 2):
-                nc.sync.dma_start(out=out_rows(d)[:, lo : lo + 2, first : first + 3 * BLK], in_=zeros)
+            a, b = AHEAD[d]
+            nc.sync.dma_start(out=out_chunk(d)[:, a:b], in_=whole[3][:, 1, 0 : b - a])
 
         def regroup(who, c, d, lo, hi):
             grouped = stage.tile([P, BLK, PACK], BF16, name="grouped", align_bytes=64)
@@ -125,15 +127,10 @@ def tile_ensemblelinear_kernel(tc, x, W, grad_out, out):
             n_cols = slice(d * BLK, (d + 1) * BLK)
             for r in range(lo, hi):
                 mx_pass(d, 1, r)
-                if r < WHOLE[d]:
-                    nc.scalar.copy(out=whole[d][:, r, n_cols], in_=accs[(d, r)][:])
-                else:
-                    nc.scalar.copy(out=part[d][:, r - WHOLE[d], :], in_=accs[(d, r)][:])
-                for a, b in STORES[d]:
-                    if b == r + 1 and b <= WHOLE[d]:
-                        nc.sync.dma_start(out=out_rows(d)[:, a:b, :], in_=whole[d][:, a:b, :])
-                    if b == r + 1 and b > WHOLE[d]:
-                        nc.sync.dma_start(out=out_rows(d)[:, a:b, n_cols], in_=part[d][:, a - WHOLE[d] : b - WHOLE[d], :])
+                nc.scalar.copy(out=whole[d][:, r, n_cols], in_=accs[(d, r)][:])
+                if r in STORES[d]:
+                    a, b = STORES[d][r]
+                    nc.sync.dma_start(out=out_chunk(d)[:, a:b], in_=whole[d][:].rearrange("p r c -> p (r c)")[:, a:b])
 
         first, second, third, last = ORDER
         urgent = [("g", 1, first, lo, hi) for lo, hi in URGENT_CUTS]
@@ -149,6 +146,10 @@ def tile_ensemblelinear_kernel(tc, x, W, grad_out, out):
             if who == "g" and c == 1:
                 if d in (third, last):
                     open_block(d)
+                if d == last:
+                    nc.scalar.copy(
+                        out=whole[first][:, :, first * BLK : (first + 1) * BLK], in_=whole[3][:, :, 0:BLK]
+                    )
                 close_rows(d, lo, hi)
 
         copied = []

@@ -24,6 +24,7 @@ BYTES = 2 * TOKENS * WIDTH * 2 + WIDTH * WIDTH * 4
 
 ORDER = (1, 2, 3, 0)
 CHUNK = ROWS * WIDTH
+ON_SCALAR = (1, 3)
 AHEAD = {0: (3 * WIDTH + BLK, CHUNK), 1: (3 * WIDTH + 2 * BLK, CHUNK), 2: (0, 2 * BLK), 3: (0, 3 * BLK)}
 STORES = {
     1: {0: (0, WIDTH), 1: (WIDTH, 2 * WIDTH), 3: (2 * WIDTH, 3 * WIDTH + 2 * BLK)},
@@ -130,7 +131,8 @@ def tile_ensemblelinear_kernel(tc, x, W, grad_out, out):
                 nc.scalar.copy(out=whole[d][:, r, n_cols], in_=accs[(d, r)][:])
                 if r in STORES[d]:
                     a, b = STORES[d][r]
-                    nc.sync.dma_start(out=out_chunk(d)[:, a:b], in_=whole[d][:].rearrange("p r c -> p (r c)")[:, a:b])
+                    queue = nc.scalar if d in ON_SCALAR else nc.sync
+                    queue.dma_start(out=out_chunk(d)[:, a:b], in_=whole[d][:].rearrange("p r c -> p (r c)")[:, a:b])
 
         first, second, third, last = ORDER
         urgent = [("g", 1, first, lo, hi) for lo, hi in URGENT_CUTS]

@@ -22,14 +22,15 @@ ROWS = BLK // P
 FLOPS = 2 * DETS * BLK * BLK * TOKENS
 BYTES = 2 * TOKENS * WIDTH * 2 + WIDTH * WIDTH * 4
 
-ORDER = (1, 2, 3, 0)
+ORDER = (3, 1, 2, 0)
 CHUNK = ROWS * WIDTH
-ON_SCALAR = (1, 3)
-AHEAD = {0: (3 * WIDTH + BLK, CHUNK), 1: (3 * WIDTH + 2 * BLK, CHUNK), 2: (0, 2 * BLK), 3: (0, 3 * BLK)}
+ON_SCALAR = (3, 2)
+RUN = WIDTH - BLK
+AHEAD = (2, 0, 1)
 STORES = {
-    1: {0: (0, WIDTH), 1: (WIDTH, 2 * WIDTH), 3: (2 * WIDTH, 3 * WIDTH + 2 * BLK)},
-    2: {3: (2 * BLK, CHUNK)},
-    3: {3: (3 * BLK, CHUNK)},
+    3: {0: (0, WIDTH + RUN), 1: (WIDTH + RUN, 2 * WIDTH + RUN), 3: (2 * WIDTH + RUN, CHUNK)},
+    1: {3: (BLK, 3 * WIDTH + 2 * BLK)},
+    2: {3: (2 * BLK, 3 * WIDTH + 3 * BLK)},
     0: {3: (0, 3 * WIDTH + BLK)},
 }
 URGENT_CUTS = ((0, 1), (1, 2), (2, 4))
@@ -77,9 +78,15 @@ def tile_ensemblelinear_kernel(tc, x, W, grad_out, out):
                 for first, width in ((0, d * BLK), ((d + 1) * BLK, WIDTH - (d + 1) * BLK)):
                     if width > 0:
                         nc.scalar.copy(out=whole[d][:, lo : lo + 2, first : first + width], in_=zeros[:, :, 0:width])
-        for d in reversed(ORDER):
-            a, b = AHEAD[d]
-            nc.sync.dma_start(out=out_chunk(d)[:, a:b], in_=whole[3][:, 1, 0 : b - a])
+        flat = out.rearrange("r c -> (r c)")
+        for d in AHEAD:
+            a = (d * BLK + ROWS - 1) * WIDTH + (d + 1) * BLK
+            runs = flat[a : a + P * CHUNK].rearrange("(m q) -> m q", q=CHUNK)[:, 0:RUN]
+            nc.sync.dma_start(out=runs, in_=whole[3][:, 1, 0:RUN])
+        for a in (BLK * WIDTH, 2 * BLK * WIDTH + BLK):
+            nc.sync.dma_start(
+                out=flat[a : a + BLK].rearrange("(p c) -> p c", p=16), in_=whole[3][0:16, 1, 0 : BLK // 16]
+            )
 
         def regroup(who, c, d, lo, hi):
             grouped = stage.tile([P, BLK, PACK], BF16, name="grouped", align_bytes=64)

@@ -50,11 +50,11 @@ def tile_ensemblelinear_kernel(tc, x, W, grad_out, out):
         codes = {}
         scales = {}
         for who in ("x", "g"):
-            codes[who] = keep.tile([P, PASSES, WIDTH], U32, name="codes_" + who, align_bytes=64)
-            scales[who] = keep.tile([P, PASSES, WIDTH], U8, name="scales_" + who, align_bytes=64)
+            codes[who] = keep.tile([P, PASSES, WIDTH], U32, name="codes_" + who, align_bytes=256)
+            scales[who] = keep.tile([P, PASSES, WIDTH], U8, name="scales_" + who, align_bytes=256)
         for c in range(PASSES):
             for who in ("x", "g"):
-                t = keep.tile([P, PACK, WIDTH], BF16, name="raw_%s%d" % (who, c), align_bytes=64)
+                t = keep.tile([P, PACK, WIDTH], BF16, name="raw_%s%d" % (who, c), align_bytes=256)
                 raw[(who, c)] = t
                 nc.sync.dma_start(
                     out=t[:],
@@ -66,7 +66,7 @@ def tile_ensemblelinear_kernel(tc, x, W, grad_out, out):
 
         whole = {}
         for d in ORDER[0:3]:
-            whole[d] = keep.tile([P, ROWS, WIDTH], F32, name="whole_%d" % d)
+            whole[d] = keep.tile([P, ROWS, WIDTH], F32, name="whole_%d" % d, align_bytes=256)
         whole[ORDER[3]] = whole[ORDER[0]]
 
         zeros = whole[3][:, 0:2, 0 : 3 * BLK]

from contextlib import ExitStack

import concourse.mybir as mybir

BF16 = mybir.dt.bfloat16
F32 = mybir.dt.float32
U32 = mybir.dt.uint32
U8 = mybir.dt.uint8
E4M3X4 = mybir.dt.float8_e4m3fn_x4
E5M2X4 = mybir.dt.float8_e5m2_x4

P = 128
PACK = 4
K_PASS = P * PACK
TOKENS = 1024
PASSES = TOKENS // K_PASS
DETS = 4
BLK = 512
WIDTH = DETS * BLK
ROWS = BLK // P

FLOPS = 2 * DETS * BLK * BLK * TOKENS
BYTES = 2 * TOKENS * WIDTH * 2 + WIDTH * WIDTH * 4

ORDER = (3, 1, 2, 0)
CHUNK = ROWS * WIDTH
ON_SCALAR = (3, 2)
RUN = WIDTH - BLK
AHEAD = (2, 0, 1)
STORES = {
    3: {0: (0, WIDTH + RUN), 1: (WIDTH + RUN, 2 * WIDTH + RUN), 3: (2 * WIDTH + RUN, CHUNK)},
    1: {3: (BLK, 3 * WIDTH + 2 * BLK)},
    2: {3: (2 * BLK, 3 * WIDTH + 3 * BLK)},
    0: {3: (0, 3 * WIDTH + BLK)},
}
URGENT_CUTS = ((0, 1), (1, 2), (2, 4))


def tile_ensemblelinear_kernel(tc, x, W, grad_out, out):
    nc = tc.nc
    with ExitStack() as ctx:
        keep = ctx.enter_context(tc.tile_pool(name="keep", bufs=1))
        stage = ctx.enter_context(tc.tile_pool(name="stage", bufs=4))
        psum = ctx.enter_context(tc.psum_pool(name="psum", bufs=8))
        ctx.enter_context(tc.manual_schedule())

        src = {"x": x, "g": grad_out}
        fmt = {"x": E4M3X4, "g": E5M2X4}
        raw = {}
        codes = {}
        scales = {}
        for who in ("x", "g"):
            codes[who] = keep.tile([P, PASSES, WIDTH], U32, name="codes_" + who, align_bytes=256)
            scales[who] = keep.tile([P, PASSES, WIDTH], U8, name="scales_" + who, align_bytes=256)
        for c in range(PASSES):
            for who in ("x", "g"):
                t = keep.tile([P, PACK, WIDTH], BF16, name="raw_%s%d" % (who, c), align_bytes=256)
                raw[(who, c)] = t
                nc.sync.dma_start(
                    out=t[:],
                    in_=src[who][c * K_PASS : (c + 1) * K_PASS, :].rearrange("(p j) w -> p j w", j=PACK),
                )

        def out_chunk(d):
            return out[d * BLK : (d + 1) * BLK, :].rearrange("(m r) c -> m (r c)", r=ROWS)

        whole = {}
        for d in ORDER[0:3]:
            whole[d] = keep.tile([P, ROWS, WIDTH], F32, name="whole_%d" % d, align_bytes=256)
        whole[ORDER[3]] = whole[ORDER[0]]

        zeros = whole[3][:, 0:2, 0 : 3 * BLK]
        nc.vector.memset(zeros, 0.0)
        for d in ORDER[0:3]:
            for lo in range(0, ROWS, 2):
                if d == 3 and lo == 0:
                    continue
                for first, width in ((0, d * BLK), ((d + 1) * BLK, WIDTH - (d + 1) * BLK)):
                    if width > 0:
                        nc.scalar.copy(out=whole[d][:, lo : lo + 2, first : first + width], in_=zeros[:, :, 0:width])
        flat = out.rearrange("r c -> (r c)")
        for d in AHEAD:
            a = (d * BLK + ROWS - 1) * WIDTH + (d + 1) * BLK
            runs = flat[a : a + P * CHUNK].rearrange("(m q) -> m q", q=CHUNK)[:, 0:RUN]
            nc.sync.dma_start(out=runs, in_=whole[3][:, 1, 0:RUN])
        for a in (BLK * WIDTH, 2 * BLK * WIDTH + BLK):
            nc.sync.dma_start(
                out=flat[a : a + BLK].rearrange("(p c) -> p c", p=16), in_=whole[3][0:16, 1, 0 : BLK // 16]
            )

        def regroup(who, c, d, lo, hi):
            grouped = stage.tile([P, BLK, PACK], BF16, name="grouped", align_bytes=64)
            block = raw[(who, c)][:, :, d * BLK : (d + 1) * BLK]
            if who == "x":
                nc.vector.tensor_copy(
                    out=grouped[:, 0 : (hi - lo) * P, :].rearrange("p (n i) t -> p n t i", i=4),
                    in_=block[:, :, lo * P : hi * P].rearrange("p t (n i) -> p n t i", i=4),
                )
            else:
                nc.vector.tensor_copy(
                    out=grouped[:, 0 : (hi - lo) * P, :].rearrange("p (r m) t -> p m t r", r=hi - lo),
                    in_=block.rearrange("p t (m r) -> p m t r", r=ROWS)[:, :, :, lo:hi],
                )
            return grouped

        def quantise(who, c, d, lo, hi, grouped):
            cols = slice(d * BLK + lo * P, d * BLK + hi * P)
            nc.vector.quantize_mx(
                out=codes[who][:, c, cols].bitcast(fmt[who]),
                scales=scales[who][:, c, cols],
                in_=grouped[:, 0 : (hi - lo) * P, :].rearrange("p w j -> p (w j)"),
            )

        accs = {}

        def mx_pass(d, c, r):
            m_cols = slice(d * BLK + r * P, d * BLK + (r + 1) * P)
            n_cols = slice(d * BLK, (d + 1) * BLK)
            nc.tensor.matmul_mx(
                out=accs[(d, r)][:],
                lhsT=codes["g"][:, c, m_cols].bitcast(E5M2X4),
                lhsT_scale=scales["g"][:, c, m_cols],
                rhs=codes["x"][:, c, n_cols].bitcast(E4M3X4),
                rhs_scale=scales["x"][:, c, n_cols],
                start=(c == 0),
                stop=(c == PASSES - 1),
            )

        def open_block(d):
            for r in range(ROWS):
                accs[(d, r)] = psum.tile([P, BLK], F32, name="acc")
                mx_pass(d, 0, r)

        def close_rows(d, lo, hi):
            n_cols = slice(d * BLK, (d + 1) * BLK)
            for r in range(lo, hi):
                mx_pass(d, 1, r)
                nc.scalar.copy(out=whole[d][:, r, n_cols], in_=accs[(d, r)][:])
                if r in STORES[d]:
                    a, b = STORES[d][r]
                    queue = nc.scalar if d in ON_SCALAR else nc.sync
                    queue.dma_start(out=out_chunk(d)[:, a:b], in_=whole[d][:].rearrange("p r c -> p (r c)")[:, a:b])

        first, second, third, last = ORDER
        urgent = [("g", 1, first, lo, hi) for lo, hi in URGENT_CUTS]
        early = [("x", 0, first), ("x", 0, second), ("x", 0, third), ("g", 0, first), ("g", 0, second)]
        early += [("x", 1, first), ("x", 1, second)]
        late = [("g", 1, second), ("g", 0, third), ("x", 1, third), ("g", 1, third)]
        late += [("x", 0, last), ("g", 0, last), ("x", 1, last), ("g", 1, last)]
        chunks = [chunk + (0, ROWS) for chunk in early] + urgent + [chunk + (0, ROWS) for chunk in late]

        def after(who, c, d, lo, hi):
            if who == "g" and c == 0 and d in (first, second):
                open_block(d)
            if who == "g" and c == 1:
                if d in (third, last):
                    open_block(d)
                if d == last:
                    nc.scalar.copy(
                        out=whole[first][:, :, first * BLK : (first + 1) * BLK], in_=whole[3][:, :, 0:BLK]
                    )
                close_rows(d, lo, hi)

        copied = []

        def quantise_all_but(n):
            while len(copied) > n:
                oldest = copied.pop(0)
                quantise(*oldest)
                after(*oldest[0:5])

        for chunk in chunks:
            if chunk in urgent:
                quantise_all_but(0)
            copied.append(chunk + (regroup(*chunk),))
            quantise_all_but(0 if chunk in urgent else 1)
        quantise_all_but(0)
